import numpy as np
import ml_dtypes

BF16 = ml_dtypes.bfloat16


def bf(x):
    return np.asarray(x, np.float32).astype(BF16)


def f32(x):
    return np.asarray(x, np.float32)


def f64(x):
    return np.asarray(x).astype(np.float64)


def striped(idx):
    return np.tile(idx.reshape(-1, 16).T, (8, 1))


D, S, P, N = 128, 4096, 256, 4096
TEMPERATURE = 0.05
SCALE = 0.05


def setup_inputs():
    return {"table": bf(SCALE * np.random.standard_normal((D, S))), "pos": bf(SCALE * np.random.standard_normal((D, P))), "offs": striped(np.random.permutation(S)[:N])}


def reference(table, pos, offs):
    idx = offs[:16].T.reshape(-1)
    return np.exp((f64(pos).T @ f64(table)[:, idx]) * (1.0 / TEMPERATURE))

@@ -1,0 +1,41 @@
+import concourse.mybir as mybir
+
+BF16, F32, U16 = mybir.dt.bfloat16, mybir.dt.float32, mybir.dt.uint16
+EXP = mybir.ActivationFunctionType.Exp
+
+FEATURES = 128
+SAMPLES = 4096
+POSITIVES = 256
+LISTED = 4096
+INVERSE_TEMPERATURE = 20.0
+
+ROWS = 128
+PIECE = 512
+PIECE_OFFSET_COLUMNS = PIECE // 16
+
+FLOPS = 2 * FEATURES * POSITIVES * LISTED
+
+
+def tile_neighbor_pairconloss_kernel(tc, table, pos, offs, out):
+    nc = tc.nc
+    with (
+        tc.tile_pool(name="held", bufs=1) as held,
+        tc.tile_pool(name="staging", bufs=4) as staging,
+        tc.psum_pool(name="banks", bufs=4) as banks,
+    ):
+        offsets = held.tile([FEATURES, LISTED // 16], U16, name="offsets")
+        nc.sync.dma_start(offsets[:], offs)
+        positives = held.tile([FEATURES, POSITIVES], BF16, name="positives")
+        nc.sync.dma_start(positives[:], pos)
+        store = held.tile([FEATURES, SAMPLES], BF16, name="store")
+        nc.sync.dma_start(store[:], table)
+
+        for block in range(POSITIVES // ROWS):
+            rows = slice(block * ROWS, (block + 1) * ROWS)
+            for piece in range(LISTED // PIECE):
+                piece_offsets = offsets[:, piece * PIECE_OFFSET_COLUMNS : (piece + 1) * PIECE_OFFSET_COLUMNS]
+                similarities = banks.tile([ROWS, PIECE], F32, name="similarities")
+                nc.tensor.matmul(similarities[:], positives[:, rows], store[:].indirect(piece_offsets))
+                exponentiated = staging.tile([ROWS, PIECE], F32, name="exponentiated")
+                nc.scalar.activation(exponentiated[:], similarities[:], EXP, scale=INVERSE_TEMPERATURE)
+                nc.sync.dma_start(out[rows, piece * PIECE : (piece + 1) * PIECE], exponentiated[:])

@@ -20,8 +20,8 @@ def tile_neighbor_pairconloss_kernel(tc, table, pos, offs, out):
     nc = tc.nc
     with (
         tc.tile_pool(name="held", bufs=1) as held,
-        tc.tile_pool(name="staging", bufs=4) as staging,
-        tc.psum_pool(name="banks", bufs=4) as banks,
+        tc.tile_pool(name="staging", bufs=16) as staging,
+        tc.psum_pool(name="banks", bufs=8) as banks,
     ):
         offsets = held.tile([FEATURES, LISTED // 16], U16, name="offsets")
         nc.sync.dma_start(offsets[:], offs)

@@ -13,6 +13,8 @@ ROWS = 128
 PIECE = 512
 PIECE_OFFSET_COLUMNS = PIECE // 16
 
+WARMUP_MATMULS = 10
+
 FLOPS = 2 * FEATURES * POSITIVES * LISTED
 
 
@@ -21,7 +23,8 @@ def tile_neighbor_pairconloss_kernel(tc, table, pos, offs, out):
     with (
         tc.tile_pool(name="held", bufs=1) as held,
         tc.tile_pool(name="staging", bufs=16) as staging,
-        tc.psum_pool(name="banks", bufs=8) as banks,
+        tc.psum_pool(name="banks", bufs=7) as banks,
+        tc.psum_pool(name="warm_bank", bufs=1) as warm_bank,
     ):
         offsets = held.tile([FEATURES, LISTED // 16], U16, name="offsets")
         nc.sync.dma_start(offsets[:], offs)
@@ -29,6 +32,12 @@ def tile_neighbor_pairconloss_kernel(tc, table, pos, offs, out):
         nc.sync.dma_start(positives[:], pos)
         store = held.tile([FEATURES, SAMPLES], BF16, name="store")
         nc.sync.dma_start(store[:], table)
+
+        zeros = held.tile([FEATURES, PIECE], BF16, name="zeros")
+        nc.vector.memset(zeros[:], 0.0)
+        unread = warm_bank.tile([ROWS, PIECE], F32, name="unread")
+        for warm in range(WARMUP_MATMULS):
+            nc.tensor.matmul(unread[:], zeros[:, 0:ROWS], zeros[:])
 
         for block in range(POSITIVES // ROWS):
             rows = slice(block * ROWS, (block + 1) * ROWS)

@@ -13,8 +13,6 @@ ROWS = 128
 PIECE = 512
 PIECE_OFFSET_COLUMNS = PIECE // 16
 
-WARMUP_MATMULS = 10
-
 FLOPS = 2 * FEATURES * POSITIVES * LISTED
 
 
@@ -23,8 +21,7 @@ def tile_neighbor_pairconloss_kernel(tc, table, pos, offs, out):
     with (
         tc.tile_pool(name="held", bufs=1) as held,
         tc.tile_pool(name="staging", bufs=16) as staging,
-        tc.psum_pool(name="banks", bufs=7) as banks,
-        tc.psum_pool(name="warm_bank", bufs=1) as warm_bank,
+        tc.psum_pool(name="banks", bufs=8) as banks,
     ):
         offsets = held.tile([FEATURES, LISTED // 16], U16, name="offsets")
         nc.sync.dma_start(offsets[:], offs)
@@ -32,12 +29,6 @@ def tile_neighbor_pairconloss_kernel(tc, table, pos, offs, out):
         nc.sync.dma_start(positives[:], pos)
         store = held.tile([FEATURES, SAMPLES], BF16, name="store")
         nc.sync.dma_start(store[:], table)
-
-        zeros = held.tile([FEATURES, PIECE], BF16, name="zeros")
-        nc.vector.memset(zeros[:], 0.0)
-        unread = warm_bank.tile([ROWS, PIECE], F32, name="unread")
-        for warm in range(WARMUP_MATMULS):
-            nc.tensor.matmul(unread[:], zeros[:, 0:ROWS], zeros[:])
 
         for block in range(POSITIVES // ROWS):
             rows = slice(block * ROWS, (block + 1) * ROWS)
@@ -47,4 +38,5 @@ def tile_neighbor_pairconloss_kernel(tc, table, pos, offs, out):
                 nc.tensor.matmul(similarities[:], positives[:, rows], store[:].indirect(piece_offsets))
                 exponentiated = staging.tile([ROWS, PIECE], F32, name="exponentiated")
                 nc.scalar.activation(exponentiated[:], similarities[:], EXP, scale=INVERSE_TEMPERATURE)
-                nc.sync.dma_start(out[rows, piece * PIECE : (piece + 1) * PIECE], exponentiated[:])
+                store_queue = nc.sync if piece % 2 == 0 else nc.gpsimd
+                store_queue.dma_start(out[rows, piece * PIECE : (piece + 1) * PIECE], exponentiated[:])

@@ -12,6 +12,7 @@ INVERSE_TEMPERATURE = 20.0
 ROWS = 128
 PIECE = 512
 PIECE_OFFSET_COLUMNS = PIECE // 16
+PAIR = 2 * PIECE
 
 FLOPS = 2 * FEATURES * POSITIVES * LISTED
 
@@ -20,7 +21,7 @@ def tile_neighbor_pairconloss_kernel(tc, table, pos, offs, out):
     nc = tc.nc
     with (
         tc.tile_pool(name="held", bufs=1) as held,
-        tc.tile_pool(name="staging", bufs=16) as staging,
+        tc.tile_pool(name="staging", bufs=8) as staging,
         tc.psum_pool(name="banks", bufs=8) as banks,
     ):
         offsets = held.tile([FEATURES, LISTED // 16], U16, name="offsets")
@@ -32,11 +33,17 @@ def tile_neighbor_pairconloss_kernel(tc, table, pos, offs, out):
 
         for block in range(POSITIVES // ROWS):
             rows = slice(block * ROWS, (block + 1) * ROWS)
-            for piece in range(LISTED // PIECE):
-                piece_offsets = offsets[:, piece * PIECE_OFFSET_COLUMNS : (piece + 1) * PIECE_OFFSET_COLUMNS]
-                similarities = banks.tile([ROWS, PIECE], F32, name="similarities")
-                nc.tensor.matmul(similarities[:], positives[:, rows], store[:].indirect(piece_offsets))
-                exponentiated = staging.tile([ROWS, PIECE], F32, name="exponentiated")
-                nc.scalar.activation(exponentiated[:], similarities[:], EXP, scale=INVERSE_TEMPERATURE)
-                store_queue = nc.sync if piece % 2 == 0 else nc.gpsimd
-                store_queue.dma_start(out[rows, piece * PIECE : (piece + 1) * PIECE], exponentiated[:])
+            for pair in range(LISTED // PAIR):
+                exponentiated = staging.tile([ROWS, PAIR], F32, name="exponentiated")
+                for side in range(2):
+                    piece = 2 * pair + side
+                    piece_offsets = offsets[:, piece * PIECE_OFFSET_COLUMNS : (piece + 1) * PIECE_OFFSET_COLUMNS]
+                    similarities = banks.tile([ROWS, PIECE], F32, name="similarities")
+                    nc.tensor.matmul(similarities[:], positives[:, rows], store[:].indirect(piece_offsets))
+                    nc.scalar.activation(
+                        exponentiated[:, side * PIECE : (side + 1) * PIECE],
+                        similarities[:],
+                        EXP,
+                        scale=INVERSE_TEMPERATURE,
+                    )
+                nc.sync.dma_start(out[rows, pair * PAIR : (pair + 1) * PAIR], exponentiated[:])

@@ -34,6 +34,7 @@ def tile_neighbor_pairconloss_kernel(tc, table, pos, offs, out):
         for block in range(POSITIVES // ROWS):
             rows = slice(block * ROWS, (block + 1) * ROWS)
             for pair in range(LISTED // PAIR):
+                first_pair = block == 0 and pair == 0
                 exponentiated = staging.tile([ROWS, PAIR], F32, name="exponentiated")
                 for side in range(2):
                     piece = 2 * pair + side
@@ -46,4 +47,10 @@ def tile_neighbor_pairconloss_kernel(tc, table, pos, offs, out):
                         EXP,
                         scale=INVERSE_TEMPERATURE,
                     )
-                nc.sync.dma_start(out[rows, pair * PAIR : (pair + 1) * PAIR], exponentiated[:])
+                    if first_pair:
+                        nc.sync.dma_start(
+                            out[rows, piece * PIECE : (piece + 1) * PIECE],
+                            exponentiated[:, side * PIECE : (side + 1) * PIECE],
+                        )
+                if not first_pair:
+                    nc.sync.dma_start(out[rows, pair * PAIR : (pair + 1) * PAIR], exponentiated[:])

@@ -34,7 +34,7 @@ def tile_neighbor_pairconloss_kernel(tc, table, pos, offs, out):
         for block in range(POSITIVES // ROWS):
             rows = slice(block * ROWS, (block + 1) * ROWS)
             for pair in range(LISTED // PAIR):
-                first_pair = block == 0 and pair == 0
+                piece_by_piece = block == 0
                 exponentiated = staging.tile([ROWS, PAIR], F32, name="exponentiated")
                 for side in range(2):
                     piece = 2 * pair + side
@@ -47,10 +47,10 @@ def tile_neighbor_pairconloss_kernel(tc, table, pos, offs, out):
                         EXP,
                         scale=INVERSE_TEMPERATURE,
                     )
-                    if first_pair:
+                    if piece_by_piece:
                         nc.sync.dma_start(
                             out[rows, piece * PIECE : (piece + 1) * PIECE],
                             exponentiated[:, side * PIECE : (side + 1) * PIECE],
                         )
-                if not first_pair:
+                if not piece_by_piece:
                     nc.sync.dma_start(out[rows, pair * PAIR : (pair + 1) * PAIR], exponentiated[:])

@@ -26,10 +26,13 @@ def tile_neighbor_pairconloss_kernel(tc, table, pos, offs, out):
     ):
         offsets = held.tile([FEATURES, LISTED // 16], U16, name="offsets")
         nc.sync.dma_start(offsets[:], offs)
-        positives = held.tile([FEATURES, POSITIVES], BF16, name="positives")
-        nc.sync.dma_start(positives[:], pos)
+        positives = []
+        for block in range(POSITIVES // ROWS):
+            positives.append(held.tile([FEATURES, ROWS], BF16, name="positives%d" % block))
+        nc.sync.dma_start(positives[0][:], pos[:, 0:ROWS])
         store = held.tile([FEATURES, SAMPLES], BF16, name="store")
         nc.sync.dma_start(store[:], table)
+        nc.sync.dma_start(positives[1][:], pos[:, ROWS : 2 * ROWS])
 
         for block in range(POSITIVES // ROWS):
             rows = slice(block * ROWS, (block + 1) * ROWS)
@@ -40,7 +43,7 @@ def tile_neighbor_pairconloss_kernel(tc, table, pos, offs, out):
                     piece = 2 * pair + side
                     piece_offsets = offsets[:, piece * PIECE_OFFSET_COLUMNS : (piece + 1) * PIECE_OFFSET_COLUMNS]
                     similarities = banks.tile([ROWS, PIECE], F32, name="similarities")
-                    nc.tensor.matmul(similarities[:], positives[:, rows], store[:].indirect(piece_offsets))
+                    nc.tensor.matmul(similarities[:], positives[block][:], store[:].indirect(piece_offsets))
                     nc.scalar.activation(
                         exponentiated[:, side * PIECE : (side + 1) * PIECE],
                         similarities[:],

@@ -34,10 +34,10 @@ def tile_neighbor_pairconloss_kernel(tc, table, pos, offs, out):
         nc.sync.dma_start(store[:], table)
         nc.sync.dma_start(positives[1][:], pos[:, ROWS : 2 * ROWS])
 
-        for block in range(POSITIVES // ROWS):
-            rows = slice(block * ROWS, (block + 1) * ROWS)
-            for pair in range(LISTED // PAIR):
-                piece_by_piece = block == 0
+        for pair in range(LISTED // PAIR):
+            for block in range(POSITIVES // ROWS):
+                rows = slice(block * ROWS, (block + 1) * ROWS)
+                piece_by_piece = pair < LISTED // PAIR // 2
                 exponentiated = staging.tile([ROWS, PAIR], F32, name="exponentiated")
                 for side in range(2):
                     piece = 2 * pair + side

import concourse.mybir as mybir

BF16, F32, U16 = mybir.dt.bfloat16, mybir.dt.float32, mybir.dt.uint16
EXP = mybir.ActivationFunctionType.Exp

FEATURES = 128
SAMPLES = 4096
POSITIVES = 256
LISTED = 4096
INVERSE_TEMPERATURE = 20.0

ROWS = 128
PIECE = 512
PIECE_OFFSET_COLUMNS = PIECE // 16
PAIR = 2 * PIECE

FLOPS = 2 * FEATURES * POSITIVES * LISTED


def tile_neighbor_pairconloss_kernel(tc, table, pos, offs, out):
    nc = tc.nc
    with (
        tc.tile_pool(name="held", bufs=1) as held,
        tc.tile_pool(name="staging", bufs=8) as staging,
        tc.psum_pool(name="banks", bufs=8) as banks,
    ):
        offsets = held.tile([FEATURES, LISTED // 16], U16, name="offsets")
        nc.sync.dma_start(offsets[:], offs)
        positives = []
        for block in range(POSITIVES // ROWS):
            positives.append(held.tile([FEATURES, ROWS], BF16, name="positives%d" % block))
        nc.sync.dma_start(positives[0][:], pos[:, 0:ROWS])
        store = held.tile([FEATURES, SAMPLES], BF16, name="store")
        nc.sync.dma_start(store[:], table)
        nc.sync.dma_start(positives[1][:], pos[:, ROWS : 2 * ROWS])

        for pair in range(LISTED // PAIR):
            for block in range(POSITIVES // ROWS):
                rows = slice(block * ROWS, (block + 1) * ROWS)
                piece_by_piece = pair < LISTED // PAIR // 2
                exponentiated = staging.tile([ROWS, PAIR], F32, name="exponentiated")
                for side in range(2):
                    piece = 2 * pair + side
                    piece_offsets = offsets[:, piece * PIECE_OFFSET_COLUMNS : (piece + 1) * PIECE_OFFSET_COLUMNS]
                    similarities = banks.tile([ROWS, PIECE], F32, name="similarities")
                    nc.tensor.matmul(similarities[:], positives[block][:], store[:].indirect(piece_offsets))
                    nc.scalar.activation(
                        exponentiated[:, side * PIECE : (side + 1) * PIECE],
                        similarities[:],
                        EXP,
                        scale=INVERSE_TEMPERATURE,
                    )
                    if piece_by_piece:
                        nc.sync.dma_start(
                            out[rows, piece * PIECE : (piece + 1) * PIECE],
                            exponentiated[:, side * PIECE : (side + 1) * PIECE],
                        )
                if not piece_by_piece:
                    nc.sync.dma_start(out[rows, pair * PAIR : (pair + 1) * PAIR], exponentiated[:])
